import numpy as np
import ml_dtypes


def mxq(x, axis, fmt="e4m3"):
    dtype, down = {"e4m3": (ml_dtypes.float8_e4m3fn, 7), "e5m2": (ml_dtypes.float8_e5m2, 14)}[fmt]
    v = np.moveaxis(np.asarray(x, np.float32).astype(ml_dtypes.bfloat16).astype(np.float64), axis, -1)
    blocks = v.reshape(v.shape[:-1] + (-1, 32))
    amax = np.abs(blocks).max(-1, keepdims=True)
    byte = np.maximum(np.where(amax > 0, np.frexp(amax)[1] - 1 + 127, 0) - down, 1)
    scale = np.exp2(byte - 127.0)
    codes = (blocks / scale).astype(np.float32).astype(dtype).astype(np.float64)
    return np.moveaxis((codes * scale).reshape(v.shape), -1, axis)


WIDE = False


def mx_kscale(k):
    if not WIDE:
        return np.ones(k)
    levels = np.array([10, -10, 5, -5, 0])
    if k % 512:
        return np.exp2(np.random.permutation(np.resize(levels, k // 32))).repeat(32)
    a = np.empty((k // 512, 16))
    for p in range(k // 512):
        a[p, :8] = np.random.permutation(np.resize(levels, 8))
        for g in range(8):
            far = levels[np.abs(levels - a[p, g]) >= 10]
            a[p, g + 8] = far[np.random.randint(len(far))]
    return np.exp2(a.ravel()).repeat(32)


BF16 = ml_dtypes.bfloat16


def bf(x):
    return np.asarray(x, np.float32).astype(BF16)


def f64(x):
    return np.asarray(x).astype(np.float64)


B, D, S, N = 1024, 2048, 4, 128
DS = D // S


def sigmoid(v):
    return 1.0 / (1.0 + np.exp(-v))


def setup_inputs():
    s = mx_kscale(D)
    t = np.maximum(1.0 + 2.0 * np.random.standard_normal((B, N, S)), 0.0) + np.maximum(1.0 + 2.0 * np.random.standard_normal((B, N, S)), 0.0)
    return {"a": bf(t * t / (t * t).sum(axis=1, keepdims=True)),
            "vr": bf(np.random.standard_normal((N, S, DS)) * 0.5 * np.sqrt(N) * s.reshape(S, DS)),
            "h": bf(np.random.standard_normal((B, D)) * s),
            "x2g": bf(np.random.standard_normal((B, D))),
            "w_g": bf(np.random.standard_normal((D, D)) / np.sqrt(D) / s),
            "b_g": bf(np.random.standard_normal(D) * 0.3),
            "bg": bf(1.0 + 0.1 * np.random.standard_normal(1))}


def reference(a, vr, h, x2g, w_g, b_g, bg):
    hf = f64(h)
    hh = (f64(a).transpose(2, 0, 1) @ f64(vr).transpose(1, 0, 2)).transpose(1, 0, 2).reshape(B, D)
    h2g = (mxq(hf, 1, "e4m3") @ mxq(f64(w_g), 1, "e4m3").T) + f64(b_g)
    g = sigmoid(f64(x2g) + h2g + f64(bg))
    return g * hh + (1.0 - g) * hf

@@ -1,0 +1,336 @@
+from contextlib import ExitStack
+
+import concourse.mybir as mybir
+from concourse.masks import make_identity
+
+F32 = mybir.dt.float32
+BF16 = mybir.dt.bfloat16
+U32 = mybir.dt.uint32
+U8 = mybir.dt.uint8
+FP8X4 = mybir.dt.float8_e4m3fn_x4
+ADD = mybir.AluOpType.add
+SUBTRACT = mybir.AluOpType.subtract
+MULT = mybir.AluOpType.mult
+SIGMOID = mybir.ActivationFunctionType.Sigmoid
+
+P = 128
+BATCH = 1024
+FEATURES = 2048
+ROLES = 128
+SLICES = 4
+SLICE = FEATURES // SLICES
+BATCH_TILES = BATCH // P
+W_TILES = SLICE // P
+PACK = 4
+PASSES = FEATURES // (P * PACK)
+STEPS = SLICES * BATCH_TILES
+FIRST_W_ROUND = 3
+
+FLOPS = 2 * BATCH * FEATURES * FEATURES + 2 * BATCH * ROLES * FEATURES
+
+
+def subtract_on_tensor_engine(step):
+    return step % 3 != 2
+
+
+def tile_tpru_pb_kernel(tc, a, vr, h, x2g, w_g, b_g, bg, out):
+    nc = tc.nc
+    with ExitStack() as ctx:
+        const = ctx.enter_context(tc.tile_pool(name="const", bufs=1))
+        h_pool = ctx.enter_context(tc.tile_pool(name="h", bufs=BATCH_TILES))
+        h_mx_pool = ctx.enter_context(tc.tile_pool(name="h_mx", bufs=BATCH_TILES))
+        a_pool = ctx.enter_context(tc.tile_pool(name="a", bufs=BATCH_TILES // 2))
+        w_pool = ctx.enter_context(tc.tile_pool(name="w", bufs=2 * W_TILES))
+        w_mx_pool = ctx.enter_context(tc.tile_pool(name="w_mx", bufs=2))
+        slice_pool = ctx.enter_context(tc.tile_pool(name="slice", bufs=2))
+        x_pool = ctx.enter_context(tc.tile_pool(name="x", bufs=BATCH_TILES + 2))
+        stage = ctx.enter_context(tc.tile_pool(name="stage", bufs=4))
+        work = ctx.enter_context(tc.tile_pool(name="work", bufs=4))
+        out_pool = ctx.enter_context(tc.tile_pool(name="out", bufs=8))
+        psum_t = ctx.enter_context(tc.psum_pool(name="psum_t", bufs=3))
+        psum_z = ctx.enter_context(tc.psum_pool(name="psum_z", bufs=2))
+        psum_d = ctx.enter_context(tc.psum_pool(name="psum_d", bufs=2))
+        psum_b = ctx.enter_context(tc.psum_pool(name="psum_b", bufs=1))
+        ctx.enter_context(tc.manual_schedule())
+
+        ident = const.tile([P, P], F32)
+        make_identity(nc, ident[:])
+        ident_bf = const.tile([P, P], BF16)
+        make_identity(nc, ident_bf[:])
+        minus_ident = const.tile([P, P], BF16)
+        nc.vector.tensor_scalar_mul(out=minus_ident[:], in0=ident_bf[:], scalar1=-1.0)
+        bg_col = const.tile([P, 1], BF16)
+        ones = const.tile([P, P], BF16)
+        nc.vector.memset(ones[:], 1.0)
+        bias_rows = const.tile([P, FEATURES], BF16)
+        nc.vector.memset(bias_rows[:], 0.0)
+
+        h_rows = {}
+        h_codes = {}
+        h_scales = {}
+        a_rows = {}
+        roles = {}
+        w_rows = {}
+        w_codes = {}
+        w_scales = {}
+        vr_slice = {}
+        bias_bank = {}
+        difference = {}
+        x_rows = {}
+        x_biased = {}
+        h_regrouped = {}
+        w_regrouped = {}
+        z_bank = {}
+        d_bank = {}
+        gate = {}
+        product = {}
+        result = {}
+
+        def load_w(s, c):
+            rows = w_pool.tile([P, FEATURES], BF16)
+            first = s * SLICE + c * P
+            nc.sync.dma_start(out=rows[:], in_=w_g[first : first + P, :])
+            w_rows[(s, c)] = rows
+
+        def load_h(i):
+            rows = h_pool.tile([P, FEATURES], BF16)
+            nc.sync.dma_start(out=rows[:], in_=h[i * P : (i + 1) * P, :])
+            h_rows[i] = rows
+
+        def load_a(pair):
+            rows = a_pool.tile([P, 2 * ROLES * SLICES], BF16)
+            nc.sync.dma_start(
+                out=rows[:].rearrange("p (j f) -> p j f", j=2),
+                in_=a[2 * pair * P : (2 * pair + 2) * P].rearrange("(j p) n s -> p j (n s)", p=P),
+            )
+            a_rows[pair] = rows
+
+        def load_vr(s):
+            vr_s = slice_pool.tile([P, SLICE], BF16)
+            nc.sync.dma_start(out=vr_s[:], in_=vr[:, s, :])
+            vr_slice[s] = vr_s
+
+        def load_x(step):
+            s, i = divmod(step, BATCH_TILES)
+            rows = x_pool.tile([P, SLICE], BF16)
+            nc.sync.dma_start(
+                out=rows[:], in_=x2g[i * P : (i + 1) * P, s * SLICE : (s + 1) * SLICE]
+            )
+            x_rows[step] = rows
+
+        def transpose_and_regroup(rows):
+            words = rows[:].bitcast(F32)
+            regrouped = stage.tile([P, FEATURES], BF16, align_bytes=64)
+            regrouped_words = regrouped[:].bitcast(F32).rearrange(
+                "p (g r u) -> p g r u", g=PASSES, u=2
+            )
+            for half in range(2):
+                bank = psum_t.tile([P, 4 * P], F32, tag="bank")
+                for q in range(4):
+                    g, u = 2 * half + q // 2, q % 2
+                    nc.tensor.transpose(
+                        bank[:, q * P : (q + 1) * P],
+                        words[:, 2 * P * g + u : 2 * P * (g + 1) : 2],
+                        ident[:],
+                    )
+                nc.scalar.copy(
+                    out=regrouped_words[:, 2 * half : 2 * half + 2],
+                    in_=bank[:].rearrange("p (g u r) -> p g r u", g=2, u=2),
+                )
+            return regrouped
+
+        def quantise_h(i, regrouped):
+            codes = h_mx_pool.tile([P, PASSES * P], U32, align_bytes=64)
+            scales = h_mx_pool.tile([P, PASSES * P], U8, align_bytes=64)
+            nc.vector.quantize_mx(out=codes[:].bitcast(FP8X4), scales=scales[:], in_=regrouped[:])
+            h_codes[i] = codes
+            h_scales[i] = scales
+
+        def quantise_w(s, c, regrouped):
+            if c == 0:
+                codes = w_mx_pool.tile([P, PASSES * SLICE], U32, align_bytes=64)
+                scales = w_mx_pool.tile([P, PASSES * SLICE], U8, align_bytes=64)
+                w_codes[s] = codes
+                w_scales[s] = scales
+            for g in range(PASSES):
+                first = g * SLICE + c * P
+                nc.vector.quantize_mx(
+                    out=w_codes[s][:, first : first + P].bitcast(FP8X4),
+                    scales=w_scales[s][:, first : first + P],
+                    in_=regrouped[:, g * P * PACK : (g + 1) * P * PACK],
+                )
+
+        def transpose_roles(pair):
+            words = a_rows[pair][:].bitcast(F32).rearrange("p (j n w) -> p j w n", j=2, w=2)
+            bank = psum_t.tile([P, 4 * P], F32, tag="bank")
+            for j in range(2):
+                for w in range(2):
+                    c = 2 * j + w
+                    nc.tensor.transpose(bank[:, c * P : (c + 1) * P], words[:, j, w, :], ident[:])
+            by_slice = a_pool.tile([P, 2 * SLICES * P], BF16)
+            nc.scalar.copy(
+                out=by_slice[:].rearrange("p (c e b) -> p c e b", c=4, e=2),
+                in_=bank[:].bitcast(BF16).rearrange("p (c b e) -> p c e b", c=4, e=2),
+            )
+            roles[pair] = by_slice
+
+        def spread_bias(s):
+            bank = psum_b.tile([P, SLICE], F32)
+            nc.tensor.matmul(
+                out=bank[:],
+                lhsT=ones[:],
+                rhs=bias_rows[:, s * SLICE : (s + 1) * SLICE],
+                start=True,
+                stop=True,
+            )
+            bias_bank[s] = bank
+
+        def add_bias(step):
+            s = step // BATCH_TILES
+            biased = work.tile([P, SLICE], F32)
+            nc.vector.tensor_tensor(
+                out=biased[:], in0=bias_bank[s][:], in1=x_rows[step][:], op=ADD
+            )
+            x_biased[step] = biased
+
+        def multiply_state(step):
+            s, i = divmod(step, BATCH_TILES)
+            z = psum_z.tile([P, SLICE], F32)
+            for g in range(PASSES):
+                nc.tensor.matmul_mx(
+                    out=z[:],
+                    lhsT=h_codes[i][:, g * P : (g + 1) * P].bitcast(FP8X4),
+                    lhsT_scale=h_scales[i][:, g * P : (g + 1) * P],
+                    rhs=w_codes[s][:, g * SLICE : (g + 1) * SLICE].bitcast(FP8X4),
+                    rhs_scale=w_scales[s][:, g * SLICE : (g + 1) * SLICE],
+                    start=(g == 0),
+                    stop=(g == PASSES - 1),
+                )
+            z_bank[step] = z
+
+        def multiply_roles(step):
+            s, i = divmod(step, BATCH_TILES)
+            d = psum_d.tile([P, SLICE], F32)
+            first = ((i % 2) * SLICES + s) * P
+            nc.tensor.matmul(
+                out=d[:],
+                lhsT=roles[i // 2][:, first : first + P],
+                rhs=vr_slice[s][:],
+                start=True,
+                stop=not subtract_on_tensor_engine(step),
+            )
+            if subtract_on_tensor_engine(step):
+                nc.tensor.matmul(
+                    out=d[:],
+                    lhsT=minus_ident[:],
+                    rhs=h_rows[i][:, s * SLICE : (s + 1) * SLICE],
+                    start=False,
+                    stop=True,
+                )
+                difference[step] = d
+            d_bank[step] = d
+
+        def open_gate(step):
+            logits = work.tile([P, SLICE], F32)
+            nc.vector.tensor_tensor(
+                out=logits[:], in0=z_bank[step][:], in1=x_biased[step][:], op=ADD
+            )
+            g_tile = work.tile([P, SLICE], F32)
+            nc.scalar.activation(
+                out=g_tile[:], in_=logits[:], func=SIGMOID, bias=bg_col[:, 0:1], scale=1.0
+            )
+            gate[step] = g_tile
+
+        def subtract(step):
+            s, i = divmod(step, BATCH_TILES)
+            subtracted = work.tile([P, SLICE], F32)
+            nc.vector.tensor_tensor(
+                out=subtracted[:],
+                in0=d_bank[step][:],
+                in1=h_rows[i][:, s * SLICE : (s + 1) * SLICE],
+                op=SUBTRACT,
+            )
+            difference[step] = subtracted
+
+        def weigh(step):
+            weighed = work.tile([P, SLICE], F32)
+            nc.vector.tensor_tensor(
+                out=weighed[:], in0=difference[step][:], in1=gate[step][:], op=MULT
+            )
+            product[step] = weighed
+
+        def blend(step):
+            s, i = divmod(step, BATCH_TILES)
+            blended = out_pool.tile([P, SLICE], F32)
+            nc.gpsimd.tensor_tensor(
+                out=blended[:],
+                in0=product[step][:],
+                in1=h_rows[i][:, s * SLICE : (s + 1) * SLICE],
+                op=ADD,
+            )
+            result[step] = blended
+
+        def store(step):
+            s, i = divmod(step, BATCH_TILES)
+            nc.sync.dma_start(
+                out=out[i * P : (i + 1) * P, s * SLICE : (s + 1) * SLICE], in_=result[step][:]
+            )
+
+        for c in range(W_TILES):
+            load_w(0, c)
+        for i in range(BATCH_TILES):
+            load_h(i)
+            if i == 0:
+                load_vr(0)
+                nc.sync.dma_start(out=bias_rows[0:1, :], in_=b_g.rearrange("(o d) -> o d", o=1))
+                nc.sync.dma_start(out=bg_col[:], in_=bg.partition_broadcast(P))
+            if i % 2 == 0:
+                load_a(i // 2)
+            load_x(i)
+            if i >= BATCH_TILES - W_TILES:
+                load_w(1, i - (BATCH_TILES - W_TILES))
+
+        for c in range(W_TILES):
+            quantise_w(0, c, transpose_and_regroup(w_rows[(0, c)]))
+        quantise_h(0, transpose_and_regroup(h_rows[0]))
+        transpose_roles(0)
+        spread_bias(0)
+        quantise_h(1, transpose_and_regroup(h_rows[1]))
+        add_bias(0)
+
+        for n in range(STEPS + 3):
+            s, i = divmod(n, BATCH_TILES)
+            if n >= 3:
+                store(n - 3)
+            if n < STEPS - BATCH_TILES:
+                load_x(n + BATCH_TILES)
+                if i == 0:
+                    load_vr(s + 1)
+                if i >= BATCH_TILES - W_TILES and s + 2 < SLICES:
+                    load_w(s + 2, i - (BATCH_TILES - W_TILES))
+            if 0 <= n - 1 < STEPS:
+                open_gate(n - 1)
+            if 0 <= n - 2 < STEPS:
+                weigh(n - 2)
+                blend(n - 2)
+            for i_next, regrouped in h_regrouped.get(n - 1, []):
+                quantise_h(i_next, regrouped)
+            for s_next, c, regrouped in w_regrouped.get(n - 1, []):
+                quantise_w(s_next, c, regrouped)
+            if 0 <= n - 1 < STEPS and not subtract_on_tensor_engine(n - 1):
+                subtract(n - 1)
+            if n + 1 < STEPS:
+                if (n + 1) % BATCH_TILES == 0:
+                    spread_bias((n + 1) // BATCH_TILES)
+                add_bias(n + 1)
+            if n < STEPS:
+                multiply_state(n)
+            if s == 0 and i + 2 < BATCH_TILES:
+                h_regrouped[n] = [(i + 2, transpose_and_regroup(h_rows[i + 2]))]
+                if i % 2 == 0:
+                    transpose_roles((i + 2) // 2)
+            if s + 1 < SLICES and FIRST_W_ROUND <= i < FIRST_W_ROUND + W_TILES:
+                c = i - FIRST_W_ROUND
+                w_regrouped[n] = [(s + 1, c, transpose_and_regroup(w_rows[(s + 1, c)]))]
+            if n < STEPS:
+                multiply_roles(n)

@@ -139,6 +139,27 @@ def tile_tpru_pb_kernel(tc, a, vr, h, x2g, w_g, b_g, bg, out):
                 )
             return regrouped
 
+        def transpose_and_regroup_pass(s, g):
+            regrouped = stage.tile([P, FEATURES], BF16, align_bytes=64)
+            regrouped_words = regrouped[:].bitcast(F32).rearrange(
+                "p (c r u) -> p c r u", c=W_TILES, u=2
+            )
+            for half in range(2):
+                bank = psum_t.tile([P, 4 * P], F32, tag="bank")
+                for q in range(4):
+                    c, u = 2 * half + q // 2, q % 2
+                    words = w_rows[(s, c)][:].bitcast(F32)
+                    nc.tensor.transpose(
+                        bank[:, q * P : (q + 1) * P],
+                        words[:, 2 * P * g + u : 2 * P * (g + 1) : 2],
+                        ident[:],
+                    )
+                nc.scalar.copy(
+                    out=regrouped_words[:, 2 * half : 2 * half + 2],
+                    in_=bank[:].rearrange("p (c u r) -> p c r u", c=2, u=2),
+                )
+            return regrouped
+
         def quantise_h(i, regrouped):
             codes = h_mx_pool.tile([P, PASSES * P], U32, align_bytes=64)
             scales = h_mx_pool.tile([P, PASSES * P], U8, align_bytes=64)
@@ -146,12 +167,13 @@ def tile_tpru_pb_kernel(tc, a, vr, h, x2g, w_g, b_g, bg, out):
             h_codes[i] = codes
             h_scales[i] = scales
 
-        def quantise_w(s, c, regrouped):
-            if c == 0:
-                codes = w_mx_pool.tile([P, PASSES * SLICE], U32, align_bytes=64)
-                scales = w_mx_pool.tile([P, PASSES * SLICE], U8, align_bytes=64)
-                w_codes[s] = codes
-                w_scales[s] = scales
+        def allocate_w(s):
+            codes = w_mx_pool.tile([P, PASSES * SLICE], U32, align_bytes=64)
+            scales = w_mx_pool.tile([P, PASSES * SLICE], U8, align_bytes=64)
+            w_codes[s] = codes
+            w_scales[s] = scales
+
+        def quantise_w_rows(s, c, regrouped):
             for g in range(PASSES):
                 first = g * SLICE + c * P
                 nc.vector.quantize_mx(
@@ -159,6 +181,14 @@ def tile_tpru_pb_kernel(tc, a, vr, h, x2g, w_g, b_g, bg, out):
                     scales=w_scales[s][:, first : first + P],
                     in_=regrouped[:, g * P * PACK : (g + 1) * P * PACK],
                 )
+
+        def quantise_w_pass(s, g, regrouped):
+            first = g * SLICE
+            nc.vector.quantize_mx(
+                out=w_codes[s][:, first : first + SLICE].bitcast(FP8X4),
+                scales=w_scales[s][:, first : first + SLICE],
+                in_=regrouped[:],
+            )
 
         def transpose_roles(pair):
             words = a_rows[pair][:].bitcast(F32).rearrange("p (j n w) -> p j w n", j=2, w=2)
@@ -290,8 +320,9 @@ def tile_tpru_pb_kernel(tc, a, vr, h, x2g, w_g, b_g, bg, out):
             if i >= BATCH_TILES - W_TILES:
                 load_w(1, i - (BATCH_TILES - W_TILES))
 
+        allocate_w(0)
         for c in range(W_TILES):
-            quantise_w(0, c, transpose_and_regroup(w_rows[(0, c)]))
+            quantise_w_rows(0, c, transpose_and_regroup(w_rows[(0, c)]))
         quantise_h(0, transpose_and_regroup(h_rows[0]))
         transpose_roles(0)
         spread_bias(0)
@@ -315,8 +346,8 @@ def tile_tpru_pb_kernel(tc, a, vr, h, x2g, w_g, b_g, bg, out):
                 blend(n - 2)
             for i_next, regrouped in h_regrouped.get(n - 1, []):
                 quantise_h(i_next, regrouped)
-            for s_next, c, regrouped in w_regrouped.get(n - 1, []):
-                quantise_w(s_next, c, regrouped)
+            for s_next, g, regrouped in w_regrouped.get(n - 1, []):
+                quantise_w_pass(s_next, g, regrouped)
             if 0 <= n - 1 < STEPS and not subtract_on_tensor_engine(n - 1):
                 subtract(n - 1)
             if n + 1 < STEPS:
@@ -329,8 +360,10 @@ def tile_tpru_pb_kernel(tc, a, vr, h, x2g, w_g, b_g, bg, out):
                 h_regrouped[n] = [(i + 2, transpose_and_regroup(h_rows[i + 2]))]
                 if i % 2 == 0:
                     transpose_roles((i + 2) // 2)
-            if s + 1 < SLICES and FIRST_W_ROUND <= i < FIRST_W_ROUND + W_TILES:
-                c = i - FIRST_W_ROUND
-                w_regrouped[n] = [(s + 1, c, transpose_and_regroup(w_rows[(s + 1, c)]))]
+            if s + 1 < SLICES and FIRST_W_ROUND <= i < FIRST_W_ROUND + PASSES:
+                g = i - FIRST_W_ROUND
+                if g == 0:
+                    allocate_w(s + 1)
+                w_regrouped[n] = [(s + 1, g, transpose_and_regroup_pass(s + 1, g))]
             if n < STEPS:
                 multiply_roles(n)

@@ -24,13 +24,14 @@ W_TILES = SLICE // P
 PACK = 4
 PASSES = FEATURES // (P * PACK)
 STEPS = SLICES * BATCH_TILES
-FIRST_W_ROUND = 3
+STEPS_ON_TENSOR = 21
+W_ROUNDS = {1: (5, 6, 7, 7), 2: (3, 4, 5, 6), 3: (3, 4, 5, 6)}
 
 FLOPS = 2 * BATCH * FEATURES * FEATURES + 2 * BATCH * ROLES * FEATURES
 
 
 def subtract_on_tensor_engine(step):
-    return step % 3 != 2
+    return step >= STEPS - STEPS_ON_TENSOR
 
 
 def tile_tpru_pb_kernel(tc, a, vr, h, x2g, w_g, b_g, bg, out):
@@ -44,6 +45,7 @@ def tile_tpru_pb_kernel(tc, a, vr, h, x2g, w_g, b_g, bg, out):
         w_mx_pool = ctx.enter_context(tc.tile_pool(name="w_mx", bufs=2))
         slice_pool = ctx.enter_context(tc.tile_pool(name="slice", bufs=2))
         x_pool = ctx.enter_context(tc.tile_pool(name="x", bufs=BATCH_TILES + 2))
+        permuted_pool = ctx.enter_context(tc.tile_pool(name="permuted", bufs=W_TILES))
         stage = ctx.enter_context(tc.tile_pool(name="stage", bufs=4))
         work = ctx.enter_context(tc.tile_pool(name="work", bufs=4))
         out_pool = ctx.enter_context(tc.tile_pool(name="out", bufs=8))
@@ -71,6 +73,7 @@ def tile_tpru_pb_kernel(tc, a, vr, h, x2g, w_g, b_g, bg, out):
         a_rows = {}
         roles = {}
         w_rows = {}
+        w_permuted = {}
         w_codes = {}
         w_scales = {}
         vr_slice = {}
@@ -139,6 +142,20 @@ def tile_tpru_pb_kernel(tc, a, vr, h, x2g, w_g, b_g, bg, out):
                 )
             return regrouped
 
+        def permute_words(s, c):
+            permuted = permuted_pool.tile([P, FEATURES], BF16)
+            nc.scalar.copy(
+                out=permuted[:].bitcast(F32).rearrange("p (g u r) -> p g u r", g=PASSES, u=2),
+                in_=w_rows[(s, c)][:].bitcast(F32).rearrange("p (g r u) -> p g u r", g=PASSES, u=2),
+            )
+            w_permuted[(s, c)] = permuted
+
+        def words_of_pass(s, c, g, u):
+            if (s, c) in w_permuted:
+                first = (2 * g + u) * P
+                return w_permuted[(s, c)][:].bitcast(F32)[:, first : first + P]
+            return w_rows[(s, c)][:].bitcast(F32)[:, 2 * P * g + u : 2 * P * (g + 1) : 2]
+
         def transpose_and_regroup_pass(s, g):
             regrouped = stage.tile([P, FEATURES], BF16, align_bytes=64)
             regrouped_words = regrouped[:].bitcast(F32).rearrange(
@@ -148,11 +165,8 @@ def tile_tpru_pb_kernel(tc, a, vr, h, x2g, w_g, b_g, bg, out):
                 bank = psum_t.tile([P, 4 * P], F32, tag="bank")
                 for q in range(4):
                     c, u = 2 * half + q // 2, q % 2
-                    words = w_rows[(s, c)][:].bitcast(F32)
                     nc.tensor.transpose(
-                        bank[:, q * P : (q + 1) * P],
-                        words[:, 2 * P * g + u : 2 * P * (g + 1) : 2],
-                        ident[:],
+                        bank[:, q * P : (q + 1) * P], words_of_pass(s, c, g, u), ident[:]
                     )
                 nc.scalar.copy(
                     out=regrouped_words[:, 2 * half : 2 * half + 2],
@@ -197,12 +211,9 @@ def tile_tpru_pb_kernel(tc, a, vr, h, x2g, w_g, b_g, bg, out):
                 for w in range(2):
                     c = 2 * j + w
                     nc.tensor.transpose(bank[:, c * P : (c + 1) * P], words[:, j, w, :], ident[:])
-            by_slice = a_pool.tile([P, 2 * SLICES * P], BF16)
-            nc.scalar.copy(
-                out=by_slice[:].rearrange("p (c e b) -> p c e b", c=4, e=2),
-                in_=bank[:].bitcast(BF16).rearrange("p (c b e) -> p c e b", c=4, e=2),
-            )
-            roles[pair] = by_slice
+            by_word = a_pool.tile([P, 2 * SLICES * P], BF16)
+            nc.scalar.copy(out=by_word[:].bitcast(F32), in_=bank[:])
+            roles[pair] = by_word[:].rearrange("p (j w b e) -> p j w e b", j=2, w=2, e=2)
 
         def spread_bias(s):
             bank = psum_b.tile([P, SLICE], F32)
@@ -241,10 +252,9 @@ def tile_tpru_pb_kernel(tc, a, vr, h, x2g, w_g, b_g, bg, out):
         def multiply_roles(step):
             s, i = divmod(step, BATCH_TILES)
             d = psum_d.tile([P, SLICE], F32)
-            first = ((i % 2) * SLICES + s) * P
             nc.tensor.matmul(
                 out=d[:],
-                lhsT=roles[i // 2][:, first : first + P],
+                lhsT=roles[i // 2][:, i % 2, s // 2, s % 2, :],
                 rhs=vr_slice[s][:],
                 start=True,
                 stop=not subtract_on_tensor_engine(step),
@@ -339,6 +349,8 @@ def tile_tpru_pb_kernel(tc, a, vr, h, x2g, w_g, b_g, bg, out):
                     load_vr(s + 1)
                 if i >= BATCH_TILES - W_TILES and s + 2 < SLICES:
                     load_w(s + 2, i - (BATCH_TILES - W_TILES))
+            if s >= 1 and s + 1 < SLICES and i < W_TILES:
+                permute_words(s + 1, i)
             if 0 <= n - 1 < STEPS:
                 open_gate(n - 1)
             if 0 <= n - 2 < STEPS:
@@ -360,10 +372,11 @@ def tile_tpru_pb_kernel(tc, a, vr, h, x2g, w_g, b_g, bg, out):
                 h_regrouped[n] = [(i + 2, transpose_and_regroup(h_rows[i + 2]))]
                 if i % 2 == 0:
                     transpose_roles((i + 2) // 2)
-            if s + 1 < SLICES and FIRST_W_ROUND <= i < FIRST_W_ROUND + PASSES:
-                g = i - FIRST_W_ROUND
-                if g == 0:
-                    allocate_w(s + 1)
-                w_regrouped[n] = [(s + 1, g, transpose_and_regroup_pass(s + 1, g))]
+            for g in range(PASSES):
+                if s + 1 < SLICES and W_ROUNDS[s + 1][g] == i:
+                    if g == 0:
+                        allocate_w(s + 1)
+                    regrouped = transpose_and_regroup_pass(s + 1, g)
+                    w_regrouped.setdefault(n, []).append((s + 1, g, regrouped))
             if n < STEPS:
                 multiply_roles(n)

@@ -24,8 +24,9 @@ W_TILES = SLICE // P
 PACK = 4
 PASSES = FEATURES // (P * PACK)
 STEPS = SLICES * BATCH_TILES
+LAST_STEPS = 2
 STEPS_ON_TENSOR = 21
-W_ROUNDS = {1: (5, 6, 7, 7), 2: (3, 4, 5, 6), 3: (3, 4, 5, 6)}
+W_ROUNDS = {1: (6, 7, 7, 7), 2: (3, 4, 5, 6), 3: (3, 4, 5, 6)}
 
 FLOPS = 2 * BATCH * FEATURES * FEATURES + 2 * BATCH * ROLES * FEATURES
 
@@ -45,6 +46,7 @@ def tile_tpru_pb_kernel(tc, a, vr, h, x2g, w_g, b_g, bg, out):
         w_mx_pool = ctx.enter_context(tc.tile_pool(name="w_mx", bufs=2))
         slice_pool = ctx.enter_context(tc.tile_pool(name="slice", bufs=2))
         x_pool = ctx.enter_context(tc.tile_pool(name="x", bufs=BATCH_TILES + 2))
+        fence_pool = ctx.enter_context(tc.tile_pool(name="fence", bufs=2))
         permuted_pool = ctx.enter_context(tc.tile_pool(name="permuted", bufs=W_TILES))
         stage = ctx.enter_context(tc.tile_pool(name="stage", bufs=4))
         work = ctx.enter_context(tc.tile_pool(name="work", bufs=4))
@@ -82,7 +84,7 @@ def tile_tpru_pb_kernel(tc, a, vr, h, x2g, w_g, b_g, bg, out):
         x_rows = {}
         x_biased = {}
         h_regrouped = {}
-        w_regrouped = {}
+        w_to_quantise = {}
         z_bank = {}
         d_bank = {}
         gate = {}
@@ -234,20 +236,28 @@ def tile_tpru_pb_kernel(tc, a, vr, h, x2g, w_g, b_g, bg, out):
             )
             x_biased[step] = biased
 
+        def parts(step):
+            count = 2 if step >= STEPS - LAST_STEPS else 1
+            width = SLICE // count
+            return [slice(j * width, (j + 1) * width) for j in range(count)]
+
         def multiply_state(step):
             s, i = divmod(step, BATCH_TILES)
-            z = psum_z.tile([P, SLICE], F32)
-            for g in range(PASSES):
-                nc.tensor.matmul_mx(
-                    out=z[:],
-                    lhsT=h_codes[i][:, g * P : (g + 1) * P].bitcast(FP8X4),
-                    lhsT_scale=h_scales[i][:, g * P : (g + 1) * P],
-                    rhs=w_codes[s][:, g * SLICE : (g + 1) * SLICE].bitcast(FP8X4),
-                    rhs_scale=w_scales[s][:, g * SLICE : (g + 1) * SLICE],
-                    start=(g == 0),
-                    stop=(g == PASSES - 1),
-                )
-            z_bank[step] = z
+            z_bank[step] = []
+            for cols in parts(step):
+                z = psum_z.tile([P, cols.stop - cols.start], F32)
+                z_bank[step].append(z)
+                for g in range(PASSES):
+                    w_cols = slice(g * SLICE + cols.start, g * SLICE + cols.stop)
+                    nc.tensor.matmul_mx(
+                        out=z[:],
+                        lhsT=h_codes[i][:, g * P : (g + 1) * P].bitcast(FP8X4),
+                        lhsT_scale=h_scales[i][:, g * P : (g + 1) * P],
+                        rhs=w_codes[s][:, w_cols].bitcast(FP8X4),
+                        rhs_scale=w_scales[s][:, w_cols],
+                        start=(g == 0),
+                        stop=(g == PASSES - 1),
+                    )
 
         def multiply_roles(step):
             s, i = divmod(step, BATCH_TILES)
@@ -272,13 +282,21 @@ def tile_tpru_pb_kernel(tc, a, vr, h, x2g, w_g, b_g, bg, out):
 
         def open_gate(step):
             logits = work.tile([P, SLICE], F32)
-            nc.vector.tensor_tensor(
-                out=logits[:], in0=z_bank[step][:], in1=x_biased[step][:], op=ADD
-            )
             g_tile = work.tile([P, SLICE], F32)
-            nc.scalar.activation(
-                out=g_tile[:], in_=logits[:], func=SIGMOID, bias=bg_col[:, 0:1], scale=1.0
-            )
+            for cols, z in zip(parts(step), z_bank[step]):
+                nc.vector.tensor_tensor(
+                    out=logits[:, cols],
+                    in0=z[:],
+                    in1=x_biased[step][:, cols],
+                    op=ADD,
+                )
+                nc.scalar.activation(
+                    out=g_tile[:, cols],
+                    in_=logits[:, cols],
+                    func=SIGMOID,
+                    bias=bg_col[:, 0:1],
+                    scale=1.0,
+                )
             gate[step] = g_tile
 
         def subtract(step):
@@ -294,39 +312,53 @@ def tile_tpru_pb_kernel(tc, a, vr, h, x2g, w_g, b_g, bg, out):
 
         def weigh(step):
             weighed = work.tile([P, SLICE], F32)
-            nc.vector.tensor_tensor(
-                out=weighed[:], in0=difference[step][:], in1=gate[step][:], op=MULT
-            )
+            for cols in parts(step):
+                nc.vector.tensor_tensor(
+                    out=weighed[:, cols],
+                    in0=difference[step][:, cols],
+                    in1=gate[step][:, cols],
+                    op=MULT,
+                )
             product[step] = weighed
+
+        def wait_for(word):
+            copied = fence_pool.tile([P, 1], U32)
+            nc.gpsimd.tensor_copy(out=copied[:], in_=word)
 
         def blend(step):
             s, i = divmod(step, BATCH_TILES)
+            engine = nc.vector if step >= STEPS - LAST_STEPS else nc.gpsimd
             blended = out_pool.tile([P, SLICE], F32)
-            nc.gpsimd.tensor_tensor(
-                out=blended[:],
-                in0=product[step][:],
-                in1=h_rows[i][:, s * SLICE : (s + 1) * SLICE],
-                op=ADD,
-            )
+            for cols in parts(step):
+                engine.tensor_tensor(
+                    out=blended[:, cols],
+                    in0=product[step][:, cols],
+                    in1=h_rows[i][:, s * SLICE + cols.start : s * SLICE + cols.stop],
+                    op=ADD,
+                )
             result[step] = blended
 
         def store(step):
             s, i = divmod(step, BATCH_TILES)
-            nc.sync.dma_start(
-                out=out[i * P : (i + 1) * P, s * SLICE : (s + 1) * SLICE], in_=result[step][:]
-            )
+            for cols in parts(step):
+                nc.sync.dma_start(
+                    out=out[i * P : (i + 1) * P, s * SLICE + cols.start : s * SLICE + cols.stop],
+                    in_=result[step][:, cols],
+                )
 
         for c in range(W_TILES):
             load_w(0, c)
+        load_h(0)
+        load_vr(0)
+        nc.sync.dma_start(out=bias_rows[0:1, :], in_=b_g.rearrange("(o d) -> o d", o=1))
+        nc.sync.dma_start(out=bg_col[:], in_=bg.partition_broadcast(P))
+        load_a(0)
         for i in range(BATCH_TILES):
-            load_h(i)
-            if i == 0:
-                load_vr(0)
-                nc.sync.dma_start(out=bias_rows[0:1, :], in_=b_g.rearrange("(o d) -> o d", o=1))
-                nc.sync.dma_start(out=bg_col[:], in_=bg.partition_broadcast(P))
-            if i % 2 == 0:
-                load_a(i // 2)
+            if i + 1 < BATCH_TILES:
+                load_h(i + 1)
             load_x(i)
+            if i % 2 == 1 and i + 1 < BATCH_TILES:
+                load_a((i + 1) // 2)
             if i >= BATCH_TILES - W_TILES:
                 load_w(1, i - (BATCH_TILES - W_TILES))
 
@@ -355,17 +387,23 @@ def tile_tpru_pb_kernel(tc, a, vr, h, x2g, w_g, b_g, bg, out):
                 open_gate(n - 1)
             if 0 <= n - 2 < STEPS:
                 weigh(n - 2)
-                blend(n - 2)
             for i_next, regrouped in h_regrouped.get(n - 1, []):
                 quantise_h(i_next, regrouped)
-            for s_next, g, regrouped in w_regrouped.get(n - 1, []):
+            for s_next, g, regrouped in w_to_quantise.get(n, []):
                 quantise_w_pass(s_next, g, regrouped)
-            if 0 <= n - 1 < STEPS and not subtract_on_tensor_engine(n - 1):
-                subtract(n - 1)
+            if 0 <= n - 2 < STEPS:
+                if n - 1 in h_regrouped:
+                    wait_for(h_codes[h_regrouped[n - 1][-1][0]][:, 0:1])
+                if n in w_to_quantise:
+                    s_next, g, regrouped = w_to_quantise[n][-1]
+                    wait_for(w_codes[s_next][:, g * SLICE : g * SLICE + 1])
+                blend(n - 2)
             if n + 1 < STEPS:
                 if (n + 1) % BATCH_TILES == 0:
                     spread_bias((n + 1) // BATCH_TILES)
                 add_bias(n + 1)
+            if 0 <= n - 1 < STEPS and not subtract_on_tensor_engine(n - 1):
+                subtract(n - 1)
             if n < STEPS:
                 multiply_state(n)
             if s == 0 and i + 2 < BATCH_TILES:
@@ -377,6 +415,7 @@ def tile_tpru_pb_kernel(tc, a, vr, h, x2g, w_g, b_g, bg, out):
                     if g == 0:
                         allocate_w(s + 1)
                     regrouped = transpose_and_regroup_pass(s + 1, g)
-                    w_regrouped.setdefault(n, []).append((s + 1, g, regrouped))
+                    quantise_round = (s + 1) * BATCH_TILES if s == 0 else n + 1
+                    w_to_quantise.setdefault(quantise_round, []).append((s + 1, g, regrouped))
             if n < STEPS:
                 multiply_roles(n)

@@ -177,15 +177,15 @@ def tile_tpru_pb_kernel(tc, a, vr, h, x2g, w_g, b_g, bg, out):
             return regrouped
 
         def quantise_h(i, regrouped):
-            codes = h_mx_pool.tile([P, PASSES * P], U32, align_bytes=64)
-            scales = h_mx_pool.tile([P, PASSES * P], U8, align_bytes=64)
+            codes = h_mx_pool.tile([P, PASSES * P], U32, align_bytes=256)
+            scales = h_mx_pool.tile([P, PASSES * P], U8, align_bytes=256)
             nc.vector.quantize_mx(out=codes[:].bitcast(FP8X4), scales=scales[:], in_=regrouped[:])
             h_codes[i] = codes
             h_scales[i] = scales
 
         def allocate_w(s):
-            codes = w_mx_pool.tile([P, PASSES * SLICE], U32, align_bytes=64)
-            scales = w_mx_pool.tile([P, PASSES * SLICE], U8, align_bytes=64)
+            codes = w_mx_pool.tile([P, PASSES * SLICE], U32, align_bytes=256)
+            scales = w_mx_pool.tile([P, PASSES * SLICE], U8, align_bytes=256)
             w_codes[s] = codes
             w_scales[s] = scales
 

@@ -25,7 +25,7 @@ PACK = 4
 PASSES = FEATURES // (P * PACK)
 STEPS = SLICES * BATCH_TILES
 LAST_STEPS = 2
-STEPS_ON_TENSOR = 21
+STEPS_ON_TENSOR = 23
 W_ROUNDS = {1: (6, 7, 7, 7), 2: (3, 4, 5, 6), 3: (3, 4, 5, 6)}
 
 FLOPS = 2 * BATCH * FEATURES * FEATURES + 2 * BATCH * ROLES * FEATURES
@@ -68,6 +68,10 @@ def tile_tpru_pb_kernel(tc, a, vr, h, x2g, w_g, b_g, bg, out):
         nc.vector.memset(ones[:], 1.0)
         bias_rows = const.tile([P, FEATURES], BF16)
         nc.vector.memset(bias_rows[:], 0.0)
+        table_loaded = const.tile([P, 1], F32)
+        nc.scalar.activation(
+            out=table_loaded[:], in_=ones[:, 0:1], func=SIGMOID, bias=0.0, scale=1.0
+        )
 
         h_rows = {}
         h_codes = {}
@@ -262,22 +266,22 @@ def tile_tpru_pb_kernel(tc, a, vr, h, x2g, w_g, b_g, bg, out):
         def multiply_roles(step):
             s, i = divmod(step, BATCH_TILES)
             d = psum_d.tile([P, SLICE], F32)
-            nc.tensor.matmul(
-                out=d[:],
-                lhsT=roles[i // 2][:, i % 2, s // 2, s % 2, :],
-                rhs=vr_slice[s][:],
-                start=True,
-                stop=not subtract_on_tensor_engine(step),
-            )
             if subtract_on_tensor_engine(step):
                 nc.tensor.matmul(
                     out=d[:],
                     lhsT=minus_ident[:],
                     rhs=h_rows[i][:, s * SLICE : (s + 1) * SLICE],
-                    start=False,
-                    stop=True,
+                    start=True,
+                    stop=False,
                 )
                 difference[step] = d
+            nc.tensor.matmul(
+                out=d[:],
+                lhsT=roles[i // 2][:, i % 2, s // 2, s % 2, :],
+                rhs=vr_slice[s][:],
+                start=not subtract_on_tensor_engine(step),
+                stop=True,
+            )
             d_bank[step] = d
 
         def open_gate(step):

@@ -22,10 +22,11 @@ SLICE = FEATURES // SLICES
 BATCH_TILES = BATCH // P
 W_TILES = SLICE // P
 PACK = 4
+BIAS_ROWS = FEATURES // (2 * P)
 PASSES = FEATURES // (P * PACK)
 STEPS = SLICES * BATCH_TILES
 LAST_STEPS = 2
-STEPS_ON_TENSOR = 23
+STEPS_ON_TENSOR = 27
 W_ROUNDS = {1: (6, 7, 7, 7), 2: (3, 4, 5, 6), 3: (3, 4, 5, 6)}
 
 FLOPS = 2 * BATCH * FEATURES * FEATURES + 2 * BATCH * ROLES * FEATURES
@@ -45,7 +46,7 @@ def tile_tpru_pb_kernel(tc, a, vr, h, x2g, w_g, b_g, bg, out):
         w_pool = ctx.enter_context(tc.tile_pool(name="w", bufs=2 * W_TILES))
         w_mx_pool = ctx.enter_context(tc.tile_pool(name="w_mx", bufs=2))
         slice_pool = ctx.enter_context(tc.tile_pool(name="slice", bufs=2))
-        x_pool = ctx.enter_context(tc.tile_pool(name="x", bufs=BATCH_TILES + 2))
+        x_pool = ctx.enter_context(tc.tile_pool(name="x", bufs=BATCH_TILES // 2 + 2))
         fence_pool = ctx.enter_context(tc.tile_pool(name="fence", bufs=2))
         permuted_pool = ctx.enter_context(tc.tile_pool(name="permuted", bufs=W_TILES))
         stage = ctx.enter_context(tc.tile_pool(name="stage", bufs=4))
@@ -61,17 +62,16 @@ def tile_tpru_pb_kernel(tc, a, vr, h, x2g, w_g, b_g, bg, out):
         make_identity(nc, ident[:])
         ident_bf = const.tile([P, P], BF16)
         make_identity(nc, ident_bf[:])
-        minus_ident = const.tile([P, P], BF16)
-        nc.vector.tensor_scalar_mul(out=minus_ident[:], in0=ident_bf[:], scalar1=-1.0)
         bg_col = const.tile([P, 1], BF16)
-        ones = const.tile([P, P], BF16)
-        nc.vector.memset(ones[:], 1.0)
-        bias_rows = const.tile([P, FEATURES], BF16)
+        bias_rows = const.tile([P, 2 * P], BF16)
         nc.vector.memset(bias_rows[:], 0.0)
+        bias_words = const.tile([P, BIAS_ROWS], F32)
         table_loaded = const.tile([P, 1], F32)
         nc.scalar.activation(
-            out=table_loaded[:], in_=ones[:, 0:1], func=SIGMOID, bias=0.0, scale=1.0
+            out=table_loaded[:], in_=bias_rows[:, 0:1], func=SIGMOID, bias=0.0, scale=1.0
         )
+        minus_ident = const.tile([P, P], BF16)
+        nc.vector.tensor_scalar_mul(out=minus_ident[:], in0=ident_bf[:], scalar1=-1.0)
 
         h_rows = {}
         h_codes = {}
@@ -121,11 +121,15 @@ def tile_tpru_pb_kernel(tc, a, vr, h, x2g, w_g, b_g, bg, out):
 
         def load_x(step):
             s, i = divmod(step, BATCH_TILES)
-            rows = x_pool.tile([P, SLICE], BF16)
+            rows = x_pool.tile([P, 2 * SLICE], BF16)
             nc.sync.dma_start(
-                out=rows[:], in_=x2g[i * P : (i + 1) * P, s * SLICE : (s + 1) * SLICE]
+                out=rows[:].rearrange("p (j f) -> p j f", j=2),
+                in_=x2g[i * P : (i + 2) * P, s * SLICE : (s + 1) * SLICE].rearrange(
+                    "(j p) f -> p j f", p=P
+                ),
             )
-            x_rows[step] = rows
+            x_rows[step] = rows[:, 0:SLICE]
+            x_rows[step + 1] = rows[:, SLICE : 2 * SLICE]
 
         def transpose_and_regroup(rows):
             words = rows[:].bitcast(F32)
@@ -221,22 +225,29 @@ def tile_tpru_pb_kernel(tc, a, vr, h, x2g, w_g, b_g, bg, out):
             nc.scalar.copy(out=by_word[:].bitcast(F32), in_=bank[:])
             roles[pair] = by_word[:].rearrange("p (j w b e) -> p j w e b", j=2, w=2, e=2)
 
+        def turn_bias():
+            bank = psum_b.tile([P, SLICE], F32)
+            nc.tensor.transpose(bank[:, 0:P], bias_rows[:].bitcast(F32), ident[:])
+            nc.scalar.copy(out=bias_words[:], in_=bank[:, 0:BIAS_ROWS])
+
         def spread_bias(s):
             bank = psum_b.tile([P, SLICE], F32)
-            nc.tensor.matmul(
-                out=bank[:],
-                lhsT=ones[:],
-                rhs=bias_rows[:, s * SLICE : (s + 1) * SLICE],
-                start=True,
-                stop=True,
-            )
-            bias_bank[s] = bank
+            for q in range(SLICE // P):
+                r = s * BIAS_ROWS // SLICES + q
+                nc.tensor.transpose(
+                    bank[:, q * P : (q + 1) * P],
+                    bias_words[:, r : r + 1].to_broadcast([P, P]),
+                    ident[:],
+                )
+            for half in range(2):
+                cols = slice(half * SLICE, (half + 1) * SLICE)
+                bias_bank[s + half] = bank[:].bitcast(BF16)[:, cols]
 
         def add_bias(step):
             s = step // BATCH_TILES
             biased = work.tile([P, SLICE], F32)
             nc.vector.tensor_tensor(
-                out=biased[:], in0=bias_bank[s][:], in1=x_rows[step][:], op=ADD
+                out=biased[:], in0=bias_bank[s], in1=x_rows[step], op=ADD
             )
             x_biased[step] = biased
 
@@ -350,17 +361,20 @@ def tile_tpru_pb_kernel(tc, a, vr, h, x2g, w_g, b_g, bg, out):
                     in_=result[step][:, cols],
                 )
 
+        nc.scalar.dma_start(
+            out=bias_rows[0:BIAS_ROWS, :], in_=b_g.rearrange("(r f) -> r f", r=BIAS_ROWS)
+        )
+        nc.scalar.dma_start(out=bg_col[:], in_=bg.partition_broadcast(P))
         for c in range(W_TILES):
             load_w(0, c)
         load_h(0)
         load_vr(0)
-        nc.sync.dma_start(out=bias_rows[0:1, :], in_=b_g.rearrange("(o d) -> o d", o=1))
-        nc.sync.dma_start(out=bg_col[:], in_=bg.partition_broadcast(P))
         load_a(0)
         for i in range(BATCH_TILES):
             if i + 1 < BATCH_TILES:
                 load_h(i + 1)
-            load_x(i)
+            if i % 2 == 0:
+                load_x(i)
             if i % 2 == 1 and i + 1 < BATCH_TILES:
                 load_a((i + 1) // 2)
             if i >= BATCH_TILES - W_TILES:
@@ -369,6 +383,7 @@ def tile_tpru_pb_kernel(tc, a, vr, h, x2g, w_g, b_g, bg, out):
         allocate_w(0)
         for c in range(W_TILES):
             quantise_w_rows(0, c, transpose_and_regroup(w_rows[(0, c)]))
+        turn_bias()
         quantise_h(0, transpose_and_regroup(h_rows[0]))
         transpose_roles(0)
         spread_bias(0)
@@ -380,7 +395,8 @@ def tile_tpru_pb_kernel(tc, a, vr, h, x2g, w_g, b_g, bg, out):
             if n >= 3:
                 store(n - 3)
             if n < STEPS - BATCH_TILES:
-                load_x(n + BATCH_TILES)
+                if n % 2 == 0:
+                    load_x(n + BATCH_TILES)
                 if i == 0:
                     load_vr(s + 1)
                 if i >= BATCH_TILES - W_TILES and s + 2 < SLICES:
@@ -403,7 +419,7 @@ def tile_tpru_pb_kernel(tc, a, vr, h, x2g, w_g, b_g, bg, out):
                     wait_for(w_codes[s_next][:, g * SLICE : g * SLICE + 1])
                 blend(n - 2)
             if n + 1 < STEPS:
-                if (n + 1) % BATCH_TILES == 0:
+                if (n + 1) % (2 * BATCH_TILES) == 0:
                     spread_bias((n + 1) // BATCH_TILES)
                 add_bias(n + 1)
             if 0 <= n - 1 < STEPS and not subtract_on_tensor_engine(n - 1):

@@ -22,6 +22,7 @@ SLICE = FEATURES // SLICES
 BATCH_TILES = BATCH // P
 W_TILES = SLICE // P
 PACK = 4
+WEIGHT_OFFSET = 32
 BIAS_ROWS = FEATURES // (2 * P)
 PASSES = FEATURES // (P * PACK)
 STEPS = SLICES * BATCH_TILES
@@ -185,9 +186,10 @@ def tile_tpru_pb_kernel(tc, a, vr, h, x2g, w_g, b_g, bg, out):
             return regrouped
 
         def quantise_h(i, regrouped):
-            codes = h_mx_pool.tile([P, PASSES * P], U32, align_bytes=256)
+            padded = h_mx_pool.tile([P, WEIGHT_OFFSET + PASSES * P], U32, align_bytes=256)
+            codes = padded[:, WEIGHT_OFFSET:]
             scales = h_mx_pool.tile([P, PASSES * P], U8, align_bytes=256)
-            nc.vector.quantize_mx(out=codes[:].bitcast(FP8X4), scales=scales[:], in_=regrouped[:])
+            nc.vector.quantize_mx(out=codes.bitcast(FP8X4), scales=scales[:], in_=regrouped[:])
             h_codes[i] = codes
             h_scales[i] = scales
 

from contextlib import ExitStack

import concourse.mybir as mybir
from concourse.masks import make_identity

F32 = mybir.dt.float32
BF16 = mybir.dt.bfloat16
U32 = mybir.dt.uint32
U8 = mybir.dt.uint8
FP8X4 = mybir.dt.float8_e4m3fn_x4
ADD = mybir.AluOpType.add
SUBTRACT = mybir.AluOpType.subtract
MULT = mybir.AluOpType.mult
SIGMOID = mybir.ActivationFunctionType.Sigmoid

P = 128
BATCH = 1024
FEATURES = 2048
ROLES = 128
SLICES = 4
SLICE = FEATURES // SLICES
BATCH_TILES = BATCH // P
W_TILES = SLICE // P
PACK = 4
WEIGHT_OFFSET = 32
BIAS_ROWS = FEATURES // (2 * P)
PASSES = FEATURES // (P * PACK)
STEPS = SLICES * BATCH_TILES
LAST_STEPS = 2
STEPS_ON_TENSOR = 27
W_ROUNDS = {1: (6, 7, 7, 7), 2: (3, 4, 5, 6), 3: (3, 4, 5, 6)}

FLOPS = 2 * BATCH * FEATURES * FEATURES + 2 * BATCH * ROLES * FEATURES


def subtract_on_tensor_engine(step):
    return step >= STEPS - STEPS_ON_TENSOR


def tile_tpru_pb_kernel(tc, a, vr, h, x2g, w_g, b_g, bg, out):
    nc = tc.nc
    with ExitStack() as ctx:
        const = ctx.enter_context(tc.tile_pool(name="const", bufs=1))
        h_pool = ctx.enter_context(tc.tile_pool(name="h", bufs=BATCH_TILES))
        h_mx_pool = ctx.enter_context(tc.tile_pool(name="h_mx", bufs=BATCH_TILES))
        a_pool = ctx.enter_context(tc.tile_pool(name="a", bufs=BATCH_TILES // 2))
        w_pool = ctx.enter_context(tc.tile_pool(name="w", bufs=2 * W_TILES))
        w_mx_pool = ctx.enter_context(tc.tile_pool(name="w_mx", bufs=2))
        slice_pool = ctx.enter_context(tc.tile_pool(name="slice", bufs=2))
        x_pool = ctx.enter_context(tc.tile_pool(name="x", bufs=BATCH_TILES // 2 + 2))
        fence_pool = ctx.enter_context(tc.tile_pool(name="fence", bufs=2))
        permuted_pool = ctx.enter_context(tc.tile_pool(name="permuted", bufs=W_TILES))
        stage = ctx.enter_context(tc.tile_pool(name="stage", bufs=4))
        work = ctx.enter_context(tc.tile_pool(name="work", bufs=4))
        out_pool = ctx.enter_context(tc.tile_pool(name="out", bufs=8))
        psum_t = ctx.enter_context(tc.psum_pool(name="psum_t", bufs=3))
        psum_z = ctx.enter_context(tc.psum_pool(name="psum_z", bufs=2))
        psum_d = ctx.enter_context(tc.psum_pool(name="psum_d", bufs=2))
        psum_b = ctx.enter_context(tc.psum_pool(name="psum_b", bufs=1))
        ctx.enter_context(tc.manual_schedule())

        ident = const.tile([P, P], F32)
        make_identity(nc, ident[:])
        ident_bf = const.tile([P, P], BF16)
        make_identity(nc, ident_bf[:])
        bg_col = const.tile([P, 1], BF16)
        bias_rows = const.tile([P, 2 * P], BF16)
        nc.vector.memset(bias_rows[:], 0.0)
        bias_words = const.tile([P, BIAS_ROWS], F32)
        table_loaded = const.tile([P, 1], F32)
        nc.scalar.activation(
            out=table_loaded[:], in_=bias_rows[:, 0:1], func=SIGMOID, bias=0.0, scale=1.0
        )
        minus_ident = const.tile([P, P], BF16)
        nc.vector.tensor_scalar_mul(out=minus_ident[:], in0=ident_bf[:], scalar1=-1.0)

        h_rows = {}
        h_codes = {}
        h_scales = {}
        a_rows = {}
        roles = {}
        w_rows = {}
        w_permuted = {}
        w_codes = {}
        w_scales = {}
        vr_slice = {}
        bias_bank = {}
        difference = {}
        x_rows = {}
        x_biased = {}
        h_regrouped = {}
        w_to_quantise = {}
        z_bank = {}
        d_bank = {}
        gate = {}
        product = {}
        result = {}

        def load_w(s, c):
            rows = w_pool.tile([P, FEATURES], BF16)
            first = s * SLICE + c * P
            nc.sync.dma_start(out=rows[:], in_=w_g[first : first + P, :])
            w_rows[(s, c)] = rows

        def load_h(i):
            rows = h_pool.tile([P, FEATURES], BF16)
            nc.sync.dma_start(out=rows[:], in_=h[i * P : (i + 1) * P, :])
            h_rows[i] = rows

        def load_a(pair):
            rows = a_pool.tile([P, 2 * ROLES * SLICES], BF16)
            nc.sync.dma_start(
                out=rows[:].rearrange("p (j f) -> p j f", j=2),
                in_=a[2 * pair * P : (2 * pair + 2) * P].rearrange("(j p) n s -> p j (n s)", p=P),
            )
            a_rows[pair] = rows

        def load_vr(s):
            vr_s = slice_pool.tile([P, SLICE], BF16)
            nc.sync.dma_start(out=vr_s[:], in_=vr[:, s, :])
            vr_slice[s] = vr_s

        def load_x(step):
            s, i = divmod(step, BATCH_TILES)
            rows = x_pool.tile([P, 2 * SLICE], BF16)
            nc.sync.dma_start(
                out=rows[:].rearrange("p (j f) -> p j f", j=2),
                in_=x2g[i * P : (i + 2) * P, s * SLICE : (s + 1) * SLICE].rearrange(
                    "(j p) f -> p j f", p=P
                ),
            )
            x_rows[step] = rows[:, 0:SLICE]
            x_rows[step + 1] = rows[:, SLICE : 2 * SLICE]

        def transpose_and_regroup(rows):
            words = rows[:].bitcast(F32)
            regrouped = stage.tile([P, FEATURES], BF16, align_bytes=64)
            regrouped_words = regrouped[:].bitcast(F32).rearrange(
                "p (g r u) -> p g r u", g=PASSES, u=2
            )
            for half in range(2):
                bank = psum_t.tile([P, 4 * P], F32, tag="bank")
                for q in range(4):
                    g, u = 2 * half + q // 2, q % 2
                    nc.tensor.transpose(
                        bank[:, q * P : (q + 1) * P],
                        words[:, 2 * P * g + u : 2 * P * (g + 1) : 2],
                        ident[:],
                    )
                nc.scalar.copy(
                    out=regrouped_words[:, 2 * half : 2 * half + 2],
                    in_=bank[:].rearrange("p (g u r) -> p g r u", g=2, u=2),
                )
            return regrouped

        def permute_words(s, c):
            permuted = permuted_pool.tile([P, FEATURES], BF16)
            nc.scalar.copy(
                out=permuted[:].bitcast(F32).rearrange("p (g u r) -> p g u r", g=PASSES, u=2),
                in_=w_rows[(s, c)][:].bitcast(F32).rearrange("p (g r u) -> p g u r", g=PASSES, u=2),
            )
            w_permuted[(s, c)] = permuted

        def words_of_pass(s, c, g, u):
            if (s, c) in w_permuted:
                first = (2 * g + u) * P
                return w_permuted[(s, c)][:].bitcast(F32)[:, first : first + P]
            return w_rows[(s, c)][:].bitcast(F32)[:, 2 * P * g + u : 2 * P * (g + 1) : 2]

        def transpose_and_regroup_pass(s, g):
            regrouped = stage.tile([P, FEATURES], BF16, align_bytes=64)
            regrouped_words = regrouped[:].bitcast(F32).rearrange(
                "p (c r u) -> p c r u", c=W_TILES, u=2
            )
            for half in range(2):
                bank = psum_t.tile([P, 4 * P], F32, tag="bank")
                for q in range(4):
                    c, u = 2 * half + q // 2, q % 2
                    nc.tensor.transpose(
                        bank[:, q * P : (q + 1) * P], words_of_pass(s, c, g, u), ident[:]
                    )
                nc.scalar.copy(
                    out=regrouped_words[:, 2 * half : 2 * half + 2],
                    in_=bank[:].rearrange("p (c u r) -> p c r u", c=2, u=2),
                )
            return regrouped

        def quantise_h(i, regrouped):
            padded = h_mx_pool.tile([P, WEIGHT_OFFSET + PASSES * P], U32, align_bytes=256)
            codes = padded[:, WEIGHT_OFFSET:]
            scales = h_mx_pool.tile([P, PASSES * P], U8, align_bytes=256)
            nc.vector.quantize_mx(out=codes.bitcast(FP8X4), scales=scales[:], in_=regrouped[:])
            h_codes[i] = codes
            h_scales[i] = scales

        def allocate_w(s):
            codes = w_mx_pool.tile([P, PASSES * SLICE], U32, align_bytes=256)
            scales = w_mx_pool.tile([P, PASSES * SLICE], U8, align_bytes=256)
            w_codes[s] = codes
            w_scales[s] = scales

        def quantise_w_rows(s, c, regrouped):
            for g in range(PASSES):
                first = g * SLICE + c * P
                nc.vector.quantize_mx(
                    out=w_codes[s][:, first : first + P].bitcast(FP8X4),
                    scales=w_scales[s][:, first : first + P],
                    in_=regrouped[:, g * P * PACK : (g + 1) * P * PACK],
                )

        def quantise_w_pass(s, g, regrouped):
            first = g * SLICE
            nc.vector.quantize_mx(
                out=w_codes[s][:, first : first + SLICE].bitcast(FP8X4),
                scales=w_scales[s][:, first : first + SLICE],
                in_=regrouped[:],
            )

        def transpose_roles(pair):
            words = a_rows[pair][:].bitcast(F32).rearrange("p (j n w) -> p j w n", j=2, w=2)
            bank = psum_t.tile([P, 4 * P], F32, tag="bank")
            for j in range(2):
                for w in range(2):
                    c = 2 * j + w
                    nc.tensor.transpose(bank[:, c * P : (c + 1) * P], words[:, j, w, :], ident[:])
            by_word = a_pool.tile([P, 2 * SLICES * P], BF16)
            nc.scalar.copy(out=by_word[:].bitcast(F32), in_=bank[:])
            roles[pair] = by_word[:].rearrange("p (j w b e) -> p j w e b", j=2, w=2, e=2)

        def turn_bias():
            bank = psum_b.tile([P, SLICE], F32)
            nc.tensor.transpose(bank[:, 0:P], bias_rows[:].bitcast(F32), ident[:])
            nc.scalar.copy(out=bias_words[:], in_=bank[:, 0:BIAS_ROWS])

        def spread_bias(s):
            bank = psum_b.tile([P, SLICE], F32)
            for q in range(SLICE // P):
                r = s * BIAS_ROWS // SLICES + q
                nc.tensor.transpose(
                    bank[:, q * P : (q + 1) * P],
                    bias_words[:, r : r + 1].to_broadcast([P, P]),
                    ident[:],
                )
            for half in range(2):
                cols = slice(half * SLICE, (half + 1) * SLICE)
                bias_bank[s + half] = bank[:].bitcast(BF16)[:, cols]

        def add_bias(step):
            s = step // BATCH_TILES
            biased = work.tile([P, SLICE], F32)
            nc.vector.tensor_tensor(
                out=biased[:], in0=bias_bank[s], in1=x_rows[step], op=ADD
            )
            x_biased[step] = biased

        def parts(step):
            count = 2 if step >= STEPS - LAST_STEPS else 1
            width = SLICE // count
            return [slice(j * width, (j + 1) * width) for j in range(count)]

        def multiply_state(step):
            s, i = divmod(step, BATCH_TILES)
            z_bank[step] = []
            for cols in parts(step):
                z = psum_z.tile([P, cols.stop - cols.start], F32)
                z_bank[step].append(z)
                for g in range(PASSES):
                    w_cols = slice(g * SLICE + cols.start, g * SLICE + cols.stop)
                    nc.tensor.matmul_mx(
                        out=z[:],
                        lhsT=h_codes[i][:, g * P : (g + 1) * P].bitcast(FP8X4),
                        lhsT_scale=h_scales[i][:, g * P : (g + 1) * P],
                        rhs=w_codes[s][:, w_cols].bitcast(FP8X4),
                        rhs_scale=w_scales[s][:, w_cols],
                        start=(g == 0),
                        stop=(g == PASSES - 1),
                    )

        def multiply_roles(step):
            s, i = divmod(step, BATCH_TILES)
            d = psum_d.tile([P, SLICE], F32)
            if subtract_on_tensor_engine(step):
                nc.tensor.matmul(
                    out=d[:],
                    lhsT=minus_ident[:],
                    rhs=h_rows[i][:, s * SLICE : (s + 1) * SLICE],
                    start=True,
                    stop=False,
                )
                difference[step] = d
            nc.tensor.matmul(
                out=d[:],
                lhsT=roles[i // 2][:, i % 2, s // 2, s % 2, :],
                rhs=vr_slice[s][:],
                start=not subtract_on_tensor_engine(step),
                stop=True,
            )
            d_bank[step] = d

        def open_gate(step):
            logits = work.tile([P, SLICE], F32)
            g_tile = work.tile([P, SLICE], F32)
            for cols, z in zip(parts(step), z_bank[step]):
                nc.vector.tensor_tensor(
                    out=logits[:, cols],
                    in0=z[:],
                    in1=x_biased[step][:, cols],
                    op=ADD,
                )
                nc.scalar.activation(
                    out=g_tile[:, cols],
                    in_=logits[:, cols],
                    func=SIGMOID,
                    bias=bg_col[:, 0:1],
                    scale=1.0,
                )
            gate[step] = g_tile

        def subtract(step):
            s, i = divmod(step, BATCH_TILES)
            subtracted = work.tile([P, SLICE], F32)
            nc.vector.tensor_tensor(
                out=subtracted[:],
                in0=d_bank[step][:],
                in1=h_rows[i][:, s * SLICE : (s + 1) * SLICE],
                op=SUBTRACT,
            )
            difference[step] = subtracted

        def weigh(step):
            weighed = work.tile([P, SLICE], F32)
            for cols in parts(step):
                nc.vector.tensor_tensor(
                    out=weighed[:, cols],
                    in0=difference[step][:, cols],
                    in1=gate[step][:, cols],
                    op=MULT,
                )
            product[step] = weighed

        def wait_for(word):
            copied = fence_pool.tile([P, 1], U32)
            nc.gpsimd.tensor_copy(out=copied[:], in_=word)

        def blend(step):
            s, i = divmod(step, BATCH_TILES)
            engine = nc.vector if step >= STEPS - LAST_STEPS else nc.gpsimd
            blended = out_pool.tile([P, SLICE], F32)
            for cols in parts(step):
                engine.tensor_tensor(
                    out=blended[:, cols],
                    in0=product[step][:, cols],
                    in1=h_rows[i][:, s * SLICE + cols.start : s * SLICE + cols.stop],
                    op=ADD,
                )
            result[step] = blended

        def store(step):
            s, i = divmod(step, BATCH_TILES)
            for cols in parts(step):
                nc.sync.dma_start(
                    out=out[i * P : (i + 1) * P, s * SLICE + cols.start : s * SLICE + cols.stop],
                    in_=result[step][:, cols],
                )

        nc.scalar.dma_start(
            out=bias_rows[0:BIAS_ROWS, :], in_=b_g.rearrange("(r f) -> r f", r=BIAS_ROWS)
        )
        nc.scalar.dma_start(out=bg_col[:], in_=bg.partition_broadcast(P))
        for c in range(W_TILES):
            load_w(0, c)
        load_h(0)
        load_vr(0)
        load_a(0)
        for i in range(BATCH_TILES):
            if i + 1 < BATCH_TILES:
                load_h(i + 1)
            if i % 2 == 0:
                load_x(i)
            if i % 2 == 1 and i + 1 < BATCH_TILES:
                load_a((i + 1) // 2)
            if i >= BATCH_TILES - W_TILES:
                load_w(1, i - (BATCH_TILES - W_TILES))

        allocate_w(0)
        for c in range(W_TILES):
            quantise_w_rows(0, c, transpose_and_regroup(w_rows[(0, c)]))
        turn_bias()
        quantise_h(0, transpose_and_regroup(h_rows[0]))
        transpose_roles(0)
        spread_bias(0)
        quantise_h(1, transpose_and_regroup(h_rows[1]))
        add_bias(0)

        for n in range(STEPS + 3):
            s, i = divmod(n, BATCH_TILES)
            if n >= 3:
                store(n - 3)
            if n < STEPS - BATCH_TILES:
                if n % 2 == 0:
                    load_x(n + BATCH_TILES)
                if i == 0:
                    load_vr(s + 1)
                if i >= BATCH_TILES - W_TILES and s + 2 < SLICES:
                    load_w(s + 2, i - (BATCH_TILES - W_TILES))
            if s >= 1 and s + 1 < SLICES and i < W_TILES:
                permute_words(s + 1, i)
            if 0 <= n - 1 < STEPS:
                open_gate(n - 1)
            if 0 <= n - 2 < STEPS:
                weigh(n - 2)
            for i_next, regrouped in h_regrouped.get(n - 1, []):
                quantise_h(i_next, regrouped)
            for s_next, g, regrouped in w_to_quantise.get(n, []):
                quantise_w_pass(s_next, g, regrouped)
            if 0 <= n - 2 < STEPS:
                if n - 1 in h_regrouped:
                    wait_for(h_codes[h_regrouped[n - 1][-1][0]][:, 0:1])
                if n in w_to_quantise:
                    s_next, g, regrouped = w_to_quantise[n][-1]
                    wait_for(w_codes[s_next][:, g * SLICE : g * SLICE + 1])
                blend(n - 2)
            if n + 1 < STEPS:
                if (n + 1) % (2 * BATCH_TILES) == 0:
                    spread_bias((n + 1) // BATCH_TILES)
                add_bias(n + 1)
            if 0 <= n - 1 < STEPS and not subtract_on_tensor_engine(n - 1):
                subtract(n - 1)
            if n < STEPS:
                multiply_state(n)
            if s == 0 and i + 2 < BATCH_TILES:
                h_regrouped[n] = [(i + 2, transpose_and_regroup(h_rows[i + 2]))]
                if i % 2 == 0:
                    transpose_roles((i + 2) // 2)
            for g in range(PASSES):
                if s + 1 < SLICES and W_ROUNDS[s + 1][g] == i:
                    if g == 0:
                        allocate_w(s + 1)
                    regrouped = transpose_and_regroup_pass(s + 1, g)
                    quantise_round = (s + 1) * BATCH_TILES if s == 0 else n + 1
                    w_to_quantise.setdefault(quantise_round, []).append((s + 1, g, regrouped))
            if n < STEPS:
                multiply_roles(n)
